import numpy as np
import ml_dtypes


def mxq(x, axis, fmt="e4m3"):
    dtype, down = {"e4m3": (ml_dtypes.float8_e4m3fn, 7), "e5m2": (ml_dtypes.float8_e5m2, 14)}[fmt]
    v = np.moveaxis(np.asarray(x, np.float32).astype(ml_dtypes.bfloat16).astype(np.float64), axis, -1)
    blocks = v.reshape(v.shape[:-1] + (-1, 32))
    amax = np.abs(blocks).max(-1, keepdims=True)
    byte = np.maximum(np.where(amax > 0, np.frexp(amax)[1] - 1 + 127, 0) - down, 1)
    scale = np.exp2(byte - 127.0)
    codes = (blocks / scale).astype(np.float32).astype(dtype).astype(np.float64)
    return np.moveaxis((codes * scale).reshape(v.shape), -1, axis)


WIDE = False


def mx_kscale(k):
    if not WIDE:
        return np.ones(k)
    levels = np.array([30, -30])
    if k % 512:
        return np.exp2(np.random.permutation(np.resize(levels, k // 32))).repeat(32)
    a = np.empty((k // 512, 16))
    for p in range(k // 512):
        a[p, :8] = np.random.permutation(np.resize(levels, 8))
        for g in range(8):
            far = levels[np.abs(levels - a[p, g]) >= 10]
            a[p, g + 8] = far[np.random.randint(len(far))]
    return np.exp2(a.ravel()).repeat(32)


BF16 = ml_dtypes.bfloat16


def bf(x):
    return np.asarray(x, np.float32).astype(BF16)


def f64(x):
    return np.asarray(x).astype(np.float64)


E2M1 = np.array([0.0, 0.5, 1.0, 1.5, 2.0, 3.0, 4.0, 6.0, -0.0, -0.5, -1.0, -1.5, -2.0, -3.0, -4.0, -6.0])


def pack_weight(w, fmt):
    k, n = w.shape
    w = f64(bf(w)).reshape(k // 32, 32, n)
    amax = np.abs(w).max(1)
    if fmt == "e4m3":
        byte = np.frexp(amax)[1] - 1 + 127 - 7
    else:
        mant, ex = np.frexp(amax / 6.0)
        byte = np.where(mant > 0.5, ex, ex - 1) + 127
    byte = np.clip(np.where(amax > 0, byte, 1), 1, 254)
    scaled = (w * np.exp2(127.0 - byte)[:, None, :]).reshape(k, n).astype(np.float32)
    by_word = np.ascontiguousarray(scaled.reshape(k // 512, 128, 4, n).transpose(0, 1, 3, 2))
    if fmt == "e4m3":
        words = by_word.astype(ml_dtypes.float8_e4m3fn).view(np.uint8)
    else:
        c = by_word.astype(ml_dtypes.float4_e2m1fn).view(np.uint8) & 0xF
        words = c[..., 0::2] | (c[..., 1::2] << 4)
    return np.ascontiguousarray(words), np.ascontiguousarray(byte.astype(np.uint8).reshape(k // 512, 16, n))


def unpack_weight(words, scales, fmt):
    g, p, n, _ = words.shape
    if fmt == "e4m3":
        vals = np.ascontiguousarray(words).view(ml_dtypes.float8_e4m3fn).astype(np.float64)
    else:
        nib = np.empty((g, p, n, 4), np.uint8)
        nib[..., 0::2] = words & 0xF
        nib[..., 1::2] = words >> 4
        vals = E2M1[nib]
    vals = vals * np.repeat(np.exp2(scales.astype(np.float64) - 127.0), 8, axis=1)[..., None]
    return vals.transpose(0, 1, 3, 2).reshape(g * 512, n)

def pack4(w):
    words, scales = pack_weight(w, "e2m1")
    return words.reshape(words.shape[0], 128, -1), scales


def unpack4(words, scales):
    return unpack_weight(words.reshape(words.shape[0], 128, -1, 2), scales, "e2m1")


B, S, D, H, DH = 2, 256, 2048, 16, 128
ROPE_BASE = 10000.0


def rope_tables():
    inv_freq = 1.0 / (ROPE_BASE ** (f64(np.arange(0, DH, 2)) / DH))
    freqs = f64(np.arange(S))[:, None] * inv_freq[None, :]
    return np.cos(freqs), np.sin(freqs)


def rope_interleaved(t, cos, sin):
    x1 = t[..., 0::2]
    x2 = t[..., 1::2]
    c = cos[None, :, None, :]
    s_ = sin[None, :, None, :]
    even = x1 * c - x2 * s_
    odd = x1 * s_ + x2 * c
    return np.stack((even, odd), axis=-1).reshape(t.shape)


def setup_inputs():
    s = mx_kscale(D)
    x = bf(np.random.standard_normal((B, S, D)) * s)
    w = np.random.standard_normal((2 * H * DH, D)) / np.sqrt(D) / s[None, :]
    words, scales = pack4(np.ascontiguousarray(w.T))
    return {"x": x, "wqk_w_words": words, "wqk_w_scales": scales}


def reference(x, wqk_w_words, wqk_w_scales):
    xqk = (mxq(f64(x), 2, "e5m2") @ unpack4(wqk_w_words, wqk_w_scales)).reshape(B, S, 2, H, DH)
    cos, sin = rope_tables()
    q = rope_interleaved(xqk[:, :, 0], cos, sin).transpose(0, 2, 1, 3)
    k = rope_interleaved(xqk[:, :, 1], cos, sin).transpose(0, 2, 1, 3)
    return q, k

@@ -1,0 +1,266 @@
+import math
+from contextlib import ExitStack
+
+import concourse.mybir as mybir
+from concourse.masks import make_identity
+
+B, S, D, H, DH = 2, 256, 2048, 16, 128
+N_OUT = 2 * H * DH
+ROPE_BASE = 10000.0
+FLOPS = 2 * B * S * D * N_OUT
+
+F32 = mybir.dt.float32
+BF16 = mybir.dt.bfloat16
+I32 = mybir.dt.int32
+U32 = mybir.dt.uint32
+U8 = mybir.dt.uint8
+E5M2X4 = mybir.dt.float8_e5m2_x4
+E2M1X4 = mybir.dt.float4_e2m1fn_x4
+ALU = mybir.AluOpType
+ACT = mybir.ActivationFunctionType
+
+P = 128
+K_PASS = 512
+PASSES = D // K_PASS
+N_TILE = 512
+HEADS_PER_TILE = N_TILE // DH
+COL_TILES = N_OUT // N_TILE
+PARITIES = S // P
+TOKEN_TILES = B * PARITIES
+HALF = D // 2
+BANKS = 8
+SCALE_COLS = 1024
+W_CHUNKS = [(0, 1), (1, 2), (2, 4), (4, 6), (6, 8)]
+
+
+def tile_attention_pa_kernel(tc, x, w_words, w_scales, out_q, out_k):
+    nc = tc.nc
+    with ExitStack() as ctx:
+        keep = ctx.enter_context(tc.tile_pool(name="keep", bufs=1))
+        stage = ctx.enter_context(tc.tile_pool(name="stage", bufs=4))
+        psum = ctx.enter_context(tc.psum_pool(name="psum", bufs=1))
+        ctx.enter_context(tc.manual_schedule())
+
+        banks_taken = []
+
+        def next_bank():
+            n = len(banks_taken)
+            banks_taken.append(n)
+            return psum.tile([P, N_TILE], F32, name="bank_%d" % n, tag="bank%d" % (n % BANKS))
+
+        x_rows = x.rearrange("b (p e) d -> b e p d", e=PARITIES)
+        x_halves = {}
+
+        def load_x(t, split):
+            src = x_rows[t // PARITIES, t % PARITIES]
+            if split:
+                for h in range(2):
+                    part = keep.tile([P, HALF], BF16, name="x_%d_%d" % (t, h))
+                    nc.sync.dma_start(out=part[:], in_=src[:, h * HALF : (h + 1) * HALF])
+                    x_halves[(t, h)] = part[:]
+            else:
+                whole = keep.tile([P, D], BF16, name="x_%d" % t)
+                nc.sync.dma_start(out=whole[:], in_=src)
+                for h in range(2):
+                    x_halves[(t, h)] = whole[:, h * HALF : (h + 1) * HALF]
+
+        planes = [
+            keep.tile([P, PASSES, SCALE_COLS], U8, name="w_plane_%d" % c, align_bytes=64)
+            for c in range(N_OUT // SCALE_COLS)
+        ]
+
+        def fill_plane(c):
+            nc.vector.memset(planes[c][:].bitcast(I32), 0)
+
+        def load_plane(c):
+            cols = slice(c * SCALE_COLS, (c + 1) * SCALE_COLS)
+            for r in range(4):
+                nc.sync.dma_start(
+                    out=planes[c][r:P:32, :, :].bitcast(I32),
+                    in_=w_scales[:, r:16:4, cols].rearrange("g q n -> q g n").bitcast(I32),
+                )
+
+        w_tiles = {}
+
+        def load_w(c):
+            lo, hi = W_CHUNKS[c]
+            codes = keep.tile([P, PASSES, 2 * N_TILE * (hi - lo)], U8, name="w_%d" % c, align_bytes=64)
+            nc.sync.dma_start(
+                out=codes[:].bitcast(I32),
+                in_=w_words[:, :, 2 * N_TILE * lo : 2 * N_TILE * hi].rearrange("g p n -> p g n").bitcast(I32),
+            )
+            for j in range(lo, hi):
+                w_tiles[j] = (codes, j - lo)
+
+        ident = keep.tile([P, P], F32)
+        signed_pos = keep.tile([P, PARITIES, 2], I32)
+        turns = keep.tile([P, PARITIES, DH], F32)
+        whole_turns = keep.tile([P, 2, PARITIES * DH], I32)
+        frac = keep.tile([P, 2, PARITIES * DH], F32)
+        table = keep.tile([P, 2, PARITIES, DH], F32)
+
+        def build_tables():
+            nc.gpsimd.iota(signed_pos[:, :, 0], [[-1, PARITIES]], base=0, channel_multiplier=-PARITIES)
+            nc.gpsimd.iota(signed_pos[:, :, 1], [[1, PARITIES]], base=0, channel_multiplier=PARITIES)
+            ratio = ROPE_BASE ** (-2.0 / DH)
+            for i in range(4):
+                nc.vector.tensor_scalar(
+                    out=turns[:, :, 2 * i : 2 * i + 2], in0=signed_pos[:],
+                    scalar1=ratio**i / (2 * math.pi), scalar2=None, op0=ALU.mult,
+                )
+            for pairs in (4, 16):
+                for m in range(1, 4):
+                    nc.vector.tensor_scalar(
+                        out=turns[:, :, 2 * pairs * m : 2 * pairs * (m + 1)], in0=turns[:, :, : 2 * pairs],
+                        scalar1=ratio ** (pairs * m), scalar2=None, op0=ALU.mult,
+                    )
+            flat = turns[:].rearrange("p e f -> p (e f)")
+            for kind, shift in enumerate((0.25, 0.0)):
+                nc.vector.tensor_scalar(out=whole_turns[:, kind, :], in0=flat, scalar1=shift, scalar2=None, op0=ALU.add)
+            for kind, shift in enumerate((0.25, 0.0)):
+                nc.vector.scalar_tensor_tensor(
+                    out=frac[:, kind, :], in0=flat, scalar=shift, in1=whole_turns[:, kind, :],
+                    op0=ALU.add, op1=ALU.subtract,
+                )
+            nc.scalar.activation(
+                out=table[:].rearrange("p k e f -> p (k e f)"), in_=frac[:].rearrange("p k n -> p (k n)"),
+                func=ACT.Sin, scale=2 * math.pi,
+            )
+
+        grouped = {}
+        x_codes = {}
+
+        def transpose_x(t):
+            for h in range(2):
+                words = x_halves[(t, h)].bitcast(F32)
+                bank = next_bank()
+                for g in range(2):
+                    for u in range(2):
+                        nc.tensor.transpose(
+                            bank[:, (2 * g + u) * P : (2 * g + u + 1) * P],
+                            words[:, 256 * g + u : 256 * (g + 1) : 2],
+                            ident[:],
+                        )
+                k_major = stage.tile([P, HALF], BF16, name="k_major", align_bytes=64)
+                nc.scalar.copy(
+                    out=k_major[:].bitcast(F32).rearrange("p (g r u) -> p g r u", g=2, u=2),
+                    in_=bank[:].rearrange("p (g u r) -> p g r u", g=2, u=2),
+                )
+                grouped[(t, h)] = k_major
+
+        def quantize_x(t):
+            for h in range(2):
+                codes = keep.tile([P, 2 * P], U32, name="x_codes_%d_%d" % (t, h), align_bytes=64)
+                scales = keep.tile([P, 2 * P], U8, name="x_scales_%d_%d" % (t, h), align_bytes=64)
+                nc.vector.quantize_mx(out=codes[:].bitcast(E5M2X4), scales=scales[:], in_=grouped[(t, h)][:])
+                x_codes[(t, h)] = (codes, scales)
+
+        sums = {}
+
+        def multiply(t, j):
+            bank = next_bank()
+            w_codes, jj = w_tiles[j]
+            plane = planes[j * N_TILE // SCALE_COLS]
+            s0 = j * N_TILE % SCALE_COLS
+            for g in range(PASSES):
+                codes, scales = x_codes[(t, g // 2)]
+                tok = slice((g % 2) * P, (g % 2 + 1) * P)
+                nc.tensor.matmul_mx(
+                    out=bank[:],
+                    lhsT=codes[:, tok].bitcast(E5M2X4),
+                    lhsT_scale=scales[:, tok],
+                    rhs=w_codes[:, g, 2 * N_TILE * jj : 2 * N_TILE * (jj + 1)].bitcast(E2M1X4),
+                    rhs_scale=plane[:, g, s0 : s0 + N_TILE],
+                    start=(g == 0),
+                    stop=(g == PASSES - 1),
+                )
+            sums[(t, j)] = bank
+
+        terms = {}
+
+        def products(t, j):
+            b, e = divmod(t, PARITIES)
+            if (b, j) not in terms:
+                cos_term = keep.tile([P, HEADS_PER_TILE, PARITIES, DH], F32, name="rotated_%d_%d" % (b, j))
+                sin_term = stage.tile([P, HEADS_PER_TILE, PARITIES, DH], F32, name="sin_term")
+                terms[(b, j)] = (cos_term, sin_term)
+            cos_term, sin_term = terms[(b, j)]
+            bank = sums[(t, j)]
+            nc.vector.tensor_tensor(
+                out=cos_term[:, :, e, :],
+                in0=bank[:].rearrange("p (h f) -> p h f", f=DH),
+                in1=table[:, 0, e : e + 1, :].to_broadcast([P, HEADS_PER_TILE, DH]),
+                op=ALU.mult,
+            )
+            nc.vector.tensor_tensor(
+                out=sin_term[:, :, e, :].rearrange("p h (i c) -> p h i c", c=2),
+                in0=bank[:].rearrange("p (h i c) -> p h i c", h=HEADS_PER_TILE, c=2)[:, :, :, ::-1],
+                in1=table[:, 1, e : e + 1, :].to_broadcast([P, HEADS_PER_TILE, DH]).rearrange("p h (i c) -> p h i c", c=2),
+                op=ALU.mult,
+            )
+
+        def out_view(b, j):
+            dst = out_q if j < COL_TILES // 2 else out_k
+            h0 = (j % (COL_TILES // 2)) * HEADS_PER_TILE
+            return dst[b, h0 : h0 + HEADS_PER_TILE].rearrange("h (p e) f -> p h e f", e=PARITIES)
+
+        def finish(b, j):
+            cos_term, sin_term = terms[(b, j)]
+            flat = cos_term[:].rearrange("p h e f -> p (h e f)")
+            nc.gpsimd.tensor_tensor(out=flat, in0=flat, in1=sin_term[:].rearrange("p h e f -> p (h e f)"), op=ALU.add)
+            nc.sync.dma_start(
+                out=out_view(b, j).rearrange("p h e f -> p h (e f)"),
+                in_=cos_term[:].rearrange("p h e f -> p h (e f)"),
+            )
+
+        def finish_parity(engine, b, j, e):
+            cos_term, sin_term = terms[(b, j)]
+            engine.tensor_tensor(out=cos_term[:, :, e, :], in0=cos_term[:, :, e, :], in1=sin_term[:, :, e, :], op=ALU.add)
+            nc.sync.dma_start(out=out_view(b, j)[:, :, e, :], in_=cos_term[:, :, e, :])
+
+        load_x(0, split=True)
+        fill_plane(0)
+        make_identity(nc, ident[:])
+        load_plane(0)
+        load_w(0)
+        load_x(1, split=False)
+        load_w(1)
+        load_x(2, split=False)
+        load_x(3, split=False)
+        build_tables()
+        transpose_x(0)
+        quantize_x(0)
+        for c in range(1, len(planes)):
+            fill_plane(c)
+        for c in range(1, len(planes)):
+            load_plane(c)
+        for c in range(2, len(W_CHUNKS)):
+            load_w(c)
+
+        multiply(0, 0)
+        transpose_x(1)
+        products(0, 0)
+        quantize_x(1)
+        multiply(0, 1)
+        products(0, 1)
+        multiply(1, 0)
+        products(1, 0)
+        finish(0, 0)
+        transpose_x(2)
+        quantize_x(2)
+        multiply(1, 1)
+        products(1, 1)
+        finish(0, 1)
+        transpose_x(3)
+        quantize_x(3)
+        rest = [(1, 0), (1, 1)] + [(b, j) for j in range(2, COL_TILES) for b in range(B)]
+        for b, j in rest[:-1]:
+            for e in range(PARITIES):
+                multiply(PARITIES * b + e, j)
+                products(PARITIES * b + e, j)
+            finish(b, j)
+        b, j = rest[-1]
+        for e, engine in enumerate((nc.gpsimd, nc.vector)):
+            multiply(PARITIES * b + e, j)
+            products(PARITIES * b + e, j)
+            finish_parity(engine, b, j, e)

@@ -29,8 +29,9 @@ PARITIES = S // P
 TOKEN_TILES = B * PARITIES
 HALF = D // 2
 BANKS = 8
-SCALE_COLS = 1024
-W_CHUNKS = [(0, 1), (1, 2), (2, 4), (4, 6), (6, 8)]
+PLANE_TILES = [(0, 1), (1, 4), (4, 8)]
+W_CHUNKS = [(1, 2), (2, 4), (4, 6), (6, 8)]
+VECTOR_ADDS = 2
 
 
 def tile_attention_pa_kernel(tc, x, w_words, w_scales, out_q, out_k):
@@ -65,32 +66,36 @@ def tile_attention_pa_kernel(tc, x, w_words, w_scales, out_q, out_k):
                     x_halves[(t, h)] = whole[:, h * HALF : (h + 1) * HALF]
 
         planes = [
-            keep.tile([P, PASSES, SCALE_COLS], U8, name="w_plane_%d" % c, align_bytes=64)
-            for c in range(N_OUT // SCALE_COLS)
+            keep.tile([P, PASSES, (hi - lo) * N_TILE], U8, name="w_plane_%d" % lo, align_bytes=64)
+            for lo, hi in PLANE_TILES
         ]
+        w_scale = {}
 
-        def fill_plane(c):
-            nc.vector.memset(planes[c][:].bitcast(I32), 0)
+        def fill_plane(c, passes):
+            nc.vector.memset(planes[c][:, passes, :].bitcast(I32), 0)
 
         def load_plane(c):
-            cols = slice(c * SCALE_COLS, (c + 1) * SCALE_COLS)
+            lo, hi = PLANE_TILES[c]
             for r in range(4):
                 nc.sync.dma_start(
                     out=planes[c][r:P:32, :, :].bitcast(I32),
-                    in_=w_scales[:, r:16:4, cols].rearrange("g q n -> q g n").bitcast(I32),
+                    in_=w_scales[:, r:16:4, lo * N_TILE : hi * N_TILE].rearrange("g q n -> q g n").bitcast(I32),
                 )
+            for j in range(lo, hi):
+                for g in range(PASSES):
+                    w_scale[(j, g)] = planes[c][:, g, (j - lo) * N_TILE : (j - lo + 1) * N_TILE]
 
-        w_tiles = {}
+        w_code = {}
 
-        def load_w(c):
-            lo, hi = W_CHUNKS[c]
-            codes = keep.tile([P, PASSES, 2 * N_TILE * (hi - lo)], U8, name="w_%d" % c, align_bytes=64)
+        def load_w(lo, hi, g_lo, g_hi):
+            codes = keep.tile([P, g_hi - g_lo, 2 * N_TILE * (hi - lo)], U8, name="w_%d_%d" % (lo, g_lo), align_bytes=64)
             nc.sync.dma_start(
                 out=codes[:].bitcast(I32),
-                in_=w_words[:, :, 2 * N_TILE * lo : 2 * N_TILE * hi].rearrange("g p n -> p g n").bitcast(I32),
+                in_=w_words[g_lo:g_hi, :, 2 * N_TILE * lo : 2 * N_TILE * hi].rearrange("g p n -> p g n").bitcast(I32),
             )
             for j in range(lo, hi):
-                w_tiles[j] = (codes, j - lo)
+                for g in range(g_lo, g_hi):
+                    w_code[(j, g)] = codes[:, g - g_lo, 2 * N_TILE * (j - lo) : 2 * N_TILE * (j - lo + 1)]
 
         ident = keep.tile([P, P], F32)
         signed_pos = keep.tile([P, PARITIES, 2], I32)
@@ -108,7 +113,8 @@ def tile_attention_pa_kernel(tc, x, w_words, w_scales, out_q, out_k):
                     out=turns[:, :, 2 * i : 2 * i + 2], in0=signed_pos[:],
                     scalar1=ratio**i / (2 * math.pi), scalar2=None, op0=ALU.mult,
                 )
-            for pairs in (4, 16):
+            for step, pairs in enumerate((4, 16)):
+                fill_plane(1, slice(2 * step, 2 * step + 2))
                 for m in range(1, 4):
                     nc.vector.tensor_scalar(
                         out=turns[:, :, 2 * pairs * m : 2 * pairs * (m + 1)], in0=turns[:, :, : 2 * pairs],
@@ -141,7 +147,7 @@ def tile_attention_pa_kernel(tc, x, w_words, w_scales, out_q, out_k):
                             words[:, 256 * g + u : 256 * (g + 1) : 2],
                             ident[:],
                         )
-                k_major = stage.tile([P, HALF], BF16, name="k_major", align_bytes=64)
+                k_major = stage.tile([P, HALF], BF16, name="k_major", bufs=2 * TOKEN_TILES, align_bytes=64)
                 nc.scalar.copy(
                     out=k_major[:].bitcast(F32).rearrange("p (g r u) -> p g r u", g=2, u=2),
                     in_=bank[:].rearrange("p (g u r) -> p g r u", g=2, u=2),
@@ -159,9 +165,6 @@ def tile_attention_pa_kernel(tc, x, w_words, w_scales, out_q, out_k):
 
         def multiply(t, j):
             bank = next_bank()
-            w_codes, jj = w_tiles[j]
-            plane = planes[j * N_TILE // SCALE_COLS]
-            s0 = j * N_TILE % SCALE_COLS
             for g in range(PASSES):
                 codes, scales = x_codes[(t, g // 2)]
                 tok = slice((g % 2) * P, (g % 2 + 1) * P)
@@ -169,8 +172,8 @@ def tile_attention_pa_kernel(tc, x, w_words, w_scales, out_q, out_k):
                     out=bank[:],
                     lhsT=codes[:, tok].bitcast(E5M2X4),
                     lhsT_scale=scales[:, tok],
-                    rhs=w_codes[:, g, 2 * N_TILE * jj : 2 * N_TILE * (jj + 1)].bitcast(E2M1X4),
-                    rhs_scale=plane[:, g, s0 : s0 + N_TILE],
+                    rhs=w_code[(j, g)].bitcast(E2M1X4),
+                    rhs_scale=w_scale[(j, g)],
                     start=(g == 0),
                     stop=(g == PASSES - 1),
                 )
@@ -204,63 +207,42 @@ def tile_attention_pa_kernel(tc, x, w_words, w_scales, out_q, out_k):
             h0 = (j % (COL_TILES // 2)) * HEADS_PER_TILE
             return dst[b, h0 : h0 + HEADS_PER_TILE].rearrange("h (p e) f -> p h e f", e=PARITIES)
 
-        def finish(b, j):
+        def finish(engine, b, j, heads):
             cos_term, sin_term = terms[(b, j)]
-            flat = cos_term[:].rearrange("p h e f -> p (h e f)")
-            nc.gpsimd.tensor_tensor(out=flat, in0=flat, in1=sin_term[:].rearrange("p h e f -> p (h e f)"), op=ALU.add)
+            flat = cos_term[:, heads].rearrange("p h e f -> p (h e f)")
+            engine.tensor_tensor(out=flat, in0=flat, in1=sin_term[:, heads].rearrange("p h e f -> p (h e f)"), op=ALU.add)
             nc.sync.dma_start(
-                out=out_view(b, j).rearrange("p h e f -> p h (e f)"),
-                in_=cos_term[:].rearrange("p h e f -> p h (e f)"),
+                out=out_view(b, j)[:, heads].rearrange("p h e f -> p h (e f)"),
+                in_=cos_term[:, heads].rearrange("p h e f -> p h (e f)"),
             )
 
-        def finish_parity(engine, b, j, e):
-            cos_term, sin_term = terms[(b, j)]
-            engine.tensor_tensor(out=cos_term[:, :, e, :], in0=cos_term[:, :, e, :], in1=sin_term[:, :, e, :], op=ALU.add)
-            nc.sync.dma_start(out=out_view(b, j)[:, :, e, :], in_=cos_term[:, :, e, :])
-
-        load_x(0, split=True)
-        fill_plane(0)
-        make_identity(nc, ident[:])
+        for t in range(TOKEN_TILES):
+            load_x(t, split=(t == 0))
+        fill_plane(0, slice(0, PASSES))
         load_plane(0)
-        load_w(0)
-        load_x(1, split=False)
-        load_w(1)
-        load_x(2, split=False)
-        load_x(3, split=False)
+        load_w(0, 1, 0, 2)
+        load_w(0, 1, 2, 4)
         build_tables()
-        transpose_x(0)
-        quantize_x(0)
-        for c in range(1, len(planes)):
-            fill_plane(c)
-        for c in range(1, len(planes)):
-            load_plane(c)
-        for c in range(2, len(W_CHUNKS)):
-            load_w(c)
+        make_identity(nc, ident[:])
+        load_plane(1)
+        for lo, hi in W_CHUNKS[:2]:
+            load_w(lo, hi, 0, PASSES)
+        for t in range(TOKEN_TILES):
+            transpose_x(t)
+            quantize_x(t)
+            if t < 2:
+                fill_plane(2, slice(2 * t, 2 * t + 2))
+        load_plane(2)
+        for lo, hi in W_CHUNKS[2:]:
+            load_w(lo, hi, 0, PASSES)
 
-        multiply(0, 0)
-        transpose_x(1)
-        products(0, 0)
-        quantize_x(1)
-        multiply(0, 1)
-        products(0, 1)
-        multiply(1, 0)
-        products(1, 0)
-        finish(0, 0)
-        transpose_x(2)
-        quantize_x(2)
-        multiply(1, 1)
-        products(1, 1)
-        finish(0, 1)
-        transpose_x(3)
-        quantize_x(3)
-        rest = [(1, 0), (1, 1)] + [(b, j) for j in range(2, COL_TILES) for b in range(B)]
-        for b, j in rest[:-1]:
+        units = [(b, j) for j in range(COL_TILES) for b in range(B)]
+        for n, (b, j) in enumerate(units):
             for e in range(PARITIES):
                 multiply(PARITIES * b + e, j)
                 products(PARITIES * b + e, j)
-            finish(b, j)
-        b, j = rest[-1]
-        for e, engine in enumerate((nc.gpsimd, nc.vector)):
-            multiply(PARITIES * b + e, j)
-            products(PARITIES * b + e, j)
-            finish_parity(engine, b, j, e)
+            if n < len(units) - VECTOR_ADDS:
+                finish(nc.gpsimd, b, j, slice(0, HEADS_PER_TILE))
+        for b, j in units[-VECTOR_ADDS:]:
+            for h0 in range(0, HEADS_PER_TILE, 2):
+                finish(nc.vector, b, j, slice(h0, h0 + 2))

@@ -31,7 +31,8 @@ HALF = D // 2
 BANKS = 8
 PLANE_TILES = [(0, 1), (1, 4), (4, 8)]
 W_CHUNKS = [(1, 2), (2, 4), (4, 6), (6, 8)]
-VECTOR_ADDS = 2
+WIDE_ADD_TILES = range(2, 6)
+VECTOR_HEAD_PAIRS = 5
 
 
 def tile_attention_pa_kernel(tc, x, w_words, w_scales, out_q, out_k):
@@ -183,11 +184,11 @@ def tile_attention_pa_kernel(tc, x, w_words, w_scales, out_q, out_k):
 
         def products(t, j):
             b, e = divmod(t, PARITIES)
-            if (b, j) not in terms:
-                cos_term = keep.tile([P, HEADS_PER_TILE, PARITIES, DH], F32, name="rotated_%d_%d" % (b, j))
-                sin_term = stage.tile([P, HEADS_PER_TILE, PARITIES, DH], F32, name="sin_term")
-                terms[(b, j)] = (cos_term, sin_term)
-            cos_term, sin_term = terms[(b, j)]
+            if j not in terms:
+                cos_both = keep.tile([P, B, HEADS_PER_TILE, PARITIES, DH], F32, name="rotated_%d" % j)
+                sin_both = stage.tile([P, B, HEADS_PER_TILE, PARITIES, DH], F32, name="sin_term")
+                terms[j] = (cos_both, sin_both)
+            cos_term, sin_term = terms[j][0][:, b], terms[j][1][:, b]
             bank = sums[(t, j)]
             nc.vector.tensor_tensor(
                 out=cos_term[:, :, e, :],
@@ -207,14 +208,19 @@ def tile_attention_pa_kernel(tc, x, w_words, w_scales, out_q, out_k):
             h0 = (j % (COL_TILES // 2)) * HEADS_PER_TILE
             return dst[b, h0 : h0 + HEADS_PER_TILE].rearrange("h (p e) f -> p h e f", e=PARITIES)
 
-        def finish(engine, b, j, heads):
-            cos_term, sin_term = terms[(b, j)]
-            flat = cos_term[:, heads].rearrange("p h e f -> p (h e f)")
-            engine.tensor_tensor(out=flat, in0=flat, in1=sin_term[:, heads].rearrange("p h e f -> p (h e f)"), op=ALU.add)
+        def add_terms(engine, j, pick):
+            rotated, sin_both = terms[j]
+            engine.tensor_tensor(out=pick(rotated), in0=pick(rotated), in1=pick(sin_both), op=ALU.add)
+
+        def store(b, j, heads):
             nc.sync.dma_start(
                 out=out_view(b, j)[:, heads].rearrange("p h e f -> p h (e f)"),
-                in_=cos_term[:, heads].rearrange("p h e f -> p h (e f)"),
+                in_=terms[j][0][:, b, heads].rearrange("p h e f -> p h (e f)"),
             )
+
+        def finish(engine, b, j, heads):
+            add_terms(engine, j, lambda tile: tile[:, b, heads].rearrange("p h e f -> p (h e f)"))
+            store(b, j, heads)
 
         for t in range(TOKEN_TILES):
             load_x(t, split=(t == 0))
@@ -236,13 +242,25 @@ def tile_attention_pa_kernel(tc, x, w_words, w_scales, out_q, out_k):
         for lo, hi in W_CHUNKS[2:]:
             load_w(lo, hi, 0, PASSES)
 
-        units = [(b, j) for j in range(COL_TILES) for b in range(B)]
-        for n, (b, j) in enumerate(units):
-            for e in range(PARITIES):
-                multiply(PARITIES * b + e, j)
-                products(PARITIES * b + e, j)
-            if n < len(units) - VECTOR_ADDS:
-                finish(nc.gpsimd, b, j, slice(0, HEADS_PER_TILE))
-        for b, j in units[-VECTOR_ADDS:]:
-            for h0 in range(0, HEADS_PER_TILE, 2):
-                finish(nc.vector, b, j, slice(h0, h0 + 2))
+        all_heads = slice(0, HEADS_PER_TILE)
+        head_pairs = [(b, j, slice(h0, h0 + 2)) for j in range(COL_TILES) for b in range(B) for h0 in (0, 2)]
+        on_vector = head_pairs[-VECTOR_HEAD_PAIRS:]
+        for j in range(COL_TILES):
+            for b in range(B):
+                for e in range(PARITIES):
+                    multiply(PARITIES * b + e, j)
+                    products(PARITIES * b + e, j)
+                    if (b, j) == (0, 0):
+                        add_terms(nc.gpsimd, j, lambda tile: tile[:, b, :, e, :])
+                left = [piece for piece in head_pairs if piece[:2] == (b, j) and piece not in on_vector]
+                if (b, j) == (0, 0):
+                    store(b, j, all_heads)
+                elif j in WIDE_ADD_TILES:
+                    if b == B - 1:
+                        add_terms(nc.gpsimd, j, lambda tile: tile[:].rearrange("p b h e f -> p (b h e f)"))
+                        for bb in range(B):
+                            store(bb, j, all_heads)
+                elif left:
+                    finish(nc.gpsimd, b, j, slice(0, 2 * len(left)))
+        for b, j, heads in on_vector:
+            finish(nc.vector, b, j, heads)

import math
from contextlib import ExitStack

import concourse.mybir as mybir
from concourse.masks import make_identity

B, S, D, H, DH = 2, 256, 2048, 16, 128
N_OUT = 2 * H * DH
ROPE_BASE = 10000.0
FLOPS = 2 * B * S * D * N_OUT

F32 = mybir.dt.float32
BF16 = mybir.dt.bfloat16
I32 = mybir.dt.int32
U32 = mybir.dt.uint32
U8 = mybir.dt.uint8
E5M2X4 = mybir.dt.float8_e5m2_x4
E2M1X4 = mybir.dt.float4_e2m1fn_x4
ALU = mybir.AluOpType
ACT = mybir.ActivationFunctionType

P = 128
K_PASS = 512
PASSES = D // K_PASS
N_TILE = 512
HEADS_PER_TILE = N_TILE // DH
COL_TILES = N_OUT // N_TILE
PARITIES = S // P
TOKEN_TILES = B * PARITIES
HALF = D // 2
BANKS = 8
PLANE_TILES = [(0, 1), (1, 4), (4, 8)]
W_CHUNKS = [(1, 2), (2, 4), (4, 6), (6, 8)]
WIDE_ADD_TILES = range(2, 6)
VECTOR_HEAD_PAIRS = 5


def tile_attention_pa_kernel(tc, x, w_words, w_scales, out_q, out_k):
    nc = tc.nc
    with ExitStack() as ctx:
        keep = ctx.enter_context(tc.tile_pool(name="keep", bufs=1))
        stage = ctx.enter_context(tc.tile_pool(name="stage", bufs=4))
        psum = ctx.enter_context(tc.psum_pool(name="psum", bufs=1))
        ctx.enter_context(tc.manual_schedule())

        banks_taken = []

        def next_bank():
            n = len(banks_taken)
            banks_taken.append(n)
            return psum.tile([P, N_TILE], F32, name="bank_%d" % n, tag="bank%d" % (n % BANKS))

        x_rows = x.rearrange("b (p e) d -> b e p d", e=PARITIES)
        x_halves = {}

        def load_x(t, split):
            src = x_rows[t // PARITIES, t % PARITIES]
            if split:
                for h in range(2):
                    part = keep.tile([P, HALF], BF16, name="x_%d_%d" % (t, h))
                    nc.sync.dma_start(out=part[:], in_=src[:, h * HALF : (h + 1) * HALF])
                    x_halves[(t, h)] = part[:]
            else:
                whole = keep.tile([P, D], BF16, name="x_%d" % t)
                nc.sync.dma_start(out=whole[:], in_=src)
                for h in range(2):
                    x_halves[(t, h)] = whole[:, h * HALF : (h + 1) * HALF]

        planes = [
            keep.tile([P, PASSES, (hi - lo) * N_TILE], U8, name="w_plane_%d" % lo, align_bytes=64)
            for lo, hi in PLANE_TILES
        ]
        w_scale = {}

        def fill_plane(c, passes):
            nc.vector.memset(planes[c][:, passes, :].bitcast(I32), 0)

        def load_plane(c):
            lo, hi = PLANE_TILES[c]
            for r in range(4):
                nc.sync.dma_start(
                    out=planes[c][r:P:32, :, :].bitcast(I32),
                    in_=w_scales[:, r:16:4, lo * N_TILE : hi * N_TILE].rearrange("g q n -> q g n").bitcast(I32),
                )
            for j in range(lo, hi):
                for g in range(PASSES):
                    w_scale[(j, g)] = planes[c][:, g, (j - lo) * N_TILE : (j - lo + 1) * N_TILE]

        w_code = {}

        def load_w(lo, hi, g_lo, g_hi):
            codes = keep.tile([P, g_hi - g_lo, 2 * N_TILE * (hi - lo)], U8, name="w_%d_%d" % (lo, g_lo), align_bytes=64)
            nc.sync.dma_start(
                out=codes[:].bitcast(I32),
                in_=w_words[g_lo:g_hi, :, 2 * N_TILE * lo : 2 * N_TILE * hi].rearrange("g p n -> p g n").bitcast(I32),
            )
            for j in range(lo, hi):
                for g in range(g_lo, g_hi):
                    w_code[(j, g)] = codes[:, g - g_lo, 2 * N_TILE * (j - lo) : 2 * N_TILE * (j - lo + 1)]

        ident = keep.tile([P, P], F32)
        signed_pos = keep.tile([P, PARITIES, 2], I32)
        turns = keep.tile([P, PARITIES, DH], F32)
        whole_turns = keep.tile([P, 2, PARITIES * DH], I32)
        frac = keep.tile([P, 2, PARITIES * DH], F32)
        table = keep.tile([P, 2, PARITIES, DH], F32)

        def build_tables():
            nc.gpsimd.iota(signed_pos[:, :, 0], [[-1, PARITIES]], base=0, channel_multiplier=-PARITIES)
            nc.gpsimd.iota(signed_pos[:, :, 1], [[1, PARITIES]], base=0, channel_multiplier=PARITIES)
            ratio = ROPE_BASE ** (-2.0 / DH)
            for i in range(4):
                nc.vector.tensor_scalar(
                    out=turns[:, :, 2 * i : 2 * i + 2], in0=signed_pos[:],
                    scalar1=ratio**i / (2 * math.pi), scalar2=None, op0=ALU.mult,
                )
            for step, pairs in enumerate((4, 16)):
                fill_plane(1, slice(2 * step, 2 * step + 2))
                for m in range(1, 4):
                    nc.vector.tensor_scalar(
                        out=turns[:, :, 2 * pairs * m : 2 * pairs * (m + 1)], in0=turns[:, :, : 2 * pairs],
                        scalar1=ratio ** (pairs * m), scalar2=None, op0=ALU.mult,
                    )
            flat = turns[:].rearrange("p e f -> p (e f)")
            for kind, shift in enumerate((0.25, 0.0)):
                nc.vector.tensor_scalar(out=whole_turns[:, kind, :], in0=flat, scalar1=shift, scalar2=None, op0=ALU.add)
            for kind, shift in enumerate((0.25, 0.0)):
                nc.vector.scalar_tensor_tensor(
                    out=frac[:, kind, :], in0=flat, scalar=shift, in1=whole_turns[:, kind, :],
                    op0=ALU.add, op1=ALU.subtract,
                )
            nc.scalar.activation(
                out=table[:].rearrange("p k e f -> p (k e f)"), in_=frac[:].rearrange("p k n -> p (k n)"),
                func=ACT.Sin, scale=2 * math.pi,
            )

        grouped = {}
        x_codes = {}

        def transpose_x(t):
            for h in range(2):
                words = x_halves[(t, h)].bitcast(F32)
                bank = next_bank()
                for g in range(2):
                    for u in range(2):
                        nc.tensor.transpose(
                            bank[:, (2 * g + u) * P : (2 * g + u + 1) * P],
                            words[:, 256 * g + u : 256 * (g + 1) : 2],
                            ident[:],
                        )
                k_major = stage.tile([P, HALF], BF16, name="k_major", bufs=2 * TOKEN_TILES, align_bytes=64)
                nc.scalar.copy(
                    out=k_major[:].bitcast(F32).rearrange("p (g r u) -> p g r u", g=2, u=2),
                    in_=bank[:].rearrange("p (g u r) -> p g r u", g=2, u=2),
                )
                grouped[(t, h)] = k_major

        def quantize_x(t):
            for h in range(2):
                codes = keep.tile([P, 2 * P], U32, name="x_codes_%d_%d" % (t, h), align_bytes=64)
                scales = keep.tile([P, 2 * P], U8, name="x_scales_%d_%d" % (t, h), align_bytes=64)
                nc.vector.quantize_mx(out=codes[:].bitcast(E5M2X4), scales=scales[:], in_=grouped[(t, h)][:])
                x_codes[(t, h)] = (codes, scales)

        sums = {}

        def multiply(t, j):
            bank = next_bank()
            for g in range(PASSES):
                codes, scales = x_codes[(t, g // 2)]
                tok = slice((g % 2) * P, (g % 2 + 1) * P)
                nc.tensor.matmul_mx(
                    out=bank[:],
                    lhsT=codes[:, tok].bitcast(E5M2X4),
                    lhsT_scale=scales[:, tok],
                    rhs=w_code[(j, g)].bitcast(E2M1X4),
                    rhs_scale=w_scale[(j, g)],
                    start=(g == 0),
                    stop=(g == PASSES - 1),
                )
            sums[(t, j)] = bank

        terms = {}

        def products(t, j):
            b, e = divmod(t, PARITIES)
            if j not in terms:
                cos_both = keep.tile([P, B, HEADS_PER_TILE, PARITIES, DH], F32, name="rotated_%d" % j)
                sin_both = stage.tile([P, B, HEADS_PER_TILE, PARITIES, DH], F32, name="sin_term")
                terms[j] = (cos_both, sin_both)
            cos_term, sin_term = terms[j][0][:, b], terms[j][1][:, b]
            bank = sums[(t, j)]
            nc.vector.tensor_tensor(
                out=cos_term[:, :, e, :],
                in0=bank[:].rearrange("p (h f) -> p h f", f=DH),
                in1=table[:, 0, e : e + 1, :].to_broadcast([P, HEADS_PER_TILE, DH]),
                op=ALU.mult,
            )
            nc.vector.tensor_tensor(
                out=sin_term[:, :, e, :].rearrange("p h (i c) -> p h i c", c=2),
                in0=bank[:].rearrange("p (h i c) -> p h i c", h=HEADS_PER_TILE, c=2)[:, :, :, ::-1],
                in1=table[:, 1, e : e + 1, :].to_broadcast([P, HEADS_PER_TILE, DH]).rearrange("p h (i c) -> p h i c", c=2),
                op=ALU.mult,
            )

        def out_view(b, j):
            dst = out_q if j < COL_TILES // 2 else out_k
            h0 = (j % (COL_TILES // 2)) * HEADS_PER_TILE
            return dst[b, h0 : h0 + HEADS_PER_TILE].rearrange("h (p e) f -> p h e f", e=PARITIES)

        def add_terms(engine, j, pick):
            rotated, sin_both = terms[j]
            engine.tensor_tensor(out=pick(rotated), in0=pick(rotated), in1=pick(sin_both), op=ALU.add)

        def store(b, j, heads):
            nc.sync.dma_start(
                out=out_view(b, j)[:, heads].rearrange("p h e f -> p h (e f)"),
                in_=terms[j][0][:, b, heads].rearrange("p h e f -> p h (e f)"),
            )

        def finish(engine, b, j, heads):
            add_terms(engine, j, lambda tile: tile[:, b, heads].rearrange("p h e f -> p (h e f)"))
            store(b, j, heads)

        for t in range(TOKEN_TILES):
            load_x(t, split=(t == 0))
        fill_plane(0, slice(0, PASSES))
        load_plane(0)
        load_w(0, 1, 0, 2)
        load_w(0, 1, 2, 4)
        build_tables()
        make_identity(nc, ident[:])
        load_plane(1)
        for lo, hi in W_CHUNKS[:2]:
            load_w(lo, hi, 0, PASSES)
        for t in range(TOKEN_TILES):
            transpose_x(t)
            quantize_x(t)
            if t < 2:
                fill_plane(2, slice(2 * t, 2 * t + 2))
        load_plane(2)
        for lo, hi in W_CHUNKS[2:]:
            load_w(lo, hi, 0, PASSES)

        all_heads = slice(0, HEADS_PER_TILE)
        head_pairs = [(b, j, slice(h0, h0 + 2)) for j in range(COL_TILES) for b in range(B) for h0 in (0, 2)]
        on_vector = head_pairs[-VECTOR_HEAD_PAIRS:]
        for j in range(COL_TILES):
            for b in range(B):
                for e in range(PARITIES):
                    multiply(PARITIES * b + e, j)
                    products(PARITIES * b + e, j)
                    if (b, j) == (0, 0):
                        add_terms(nc.gpsimd, j, lambda tile: tile[:, b, :, e, :])
                left = [piece for piece in head_pairs if piece[:2] == (b, j) and piece not in on_vector]
                if (b, j) == (0, 0):
                    store(b, j, all_heads)
                elif j in WIDE_ADD_TILES:
                    if b == B - 1:
                        add_terms(nc.gpsimd, j, lambda tile: tile[:].rearrange("p b h e f -> p (b h e f)"))
                        for bb in range(B):
                            store(bb, j, all_heads)
                elif left:
                    finish(nc.gpsimd, b, j, slice(0, 2 * len(left)))
        for b, j, heads in on_vector:
            finish(nc.vector, b, j, heads)
